import numpy as np
import ml_dtypes


def mxq(x, axis, fmt="e4m3"):
    dtype, down = {"e4m3": (ml_dtypes.float8_e4m3fn, 7), "e5m2": (ml_dtypes.float8_e5m2, 14)}[fmt]
    v = np.moveaxis(np.asarray(x, np.float32).astype(ml_dtypes.bfloat16).astype(np.float64), axis, -1)
    blocks = v.reshape(v.shape[:-1] + (-1, 32))
    amax = np.abs(blocks).max(-1, keepdims=True)
    byte = np.maximum(np.where(amax > 0, np.frexp(amax)[1] - 1 + 127, 0) - down, 1)
    scale = np.exp2(byte - 127.0)
    codes = (blocks / scale).astype(np.float32).astype(dtype).astype(np.float64)
    return np.moveaxis((codes * scale).reshape(v.shape), -1, axis)


WIDE = False


def mx_kscale(k):
    if not WIDE:
        return np.ones(k)
    levels = np.array([20, -20, 10, -10, 0])
    a = np.random.permutation(np.resize(levels, k // 512 * 4)).reshape(k // 512, 4)
    idx = np.arange(k)
    return np.exp2(a[idx // 512, idx % 128 // 32])


BF16 = ml_dtypes.bfloat16


def bf(x):
    return np.asarray(x, np.float32).astype(BF16)


def f64(x):
    return np.asarray(x).astype(np.float64)


N, M, D, B = 256, 512, 4, 512
MD = M * D


def sigmoid(v):
    return 1.0 / (1.0 + np.exp(-v))


def diag_mask():
    return np.broadcast_to((1.0 - np.eye(M))[:, :, None], (M, M, D)).reshape(M, MD)


def tri_mask():
    return f64(np.arange(D)[:, None] < np.arange(D)[None, :])


def big_diag(w):
    w3 = w.reshape(M, M, D).copy()
    i = np.arange(M)
    w3[i, i, :] = np.random.standard_normal((M, D)) * 0.5
    return w3.reshape(M, MD)


def gates(x_t, m_t, a_t, A_fg, A_in, A_th, A_pt_blk, B_fg, B_in, B_th, b_fg, b_in, b_th):
    x, m, a = f64(x_t), f64(m_t), f64(a_t)
    gf = sigmoid(m @ f64(A_fg) + x @ f64(B_fg) + f64(b_fg))
    gi = sigmoid(m @ f64(A_in) + x @ f64(B_in) + f64(b_in))
    a3 = a.reshape(B, M, D)
    P = f64(A_pt_blk) * tri_mask()
    pt = np.zeros((B, M, D))
    for s in range(D):
        pt = pt + a3[:, :, s, None] * P[None, :, s, :]
    a_last = a3[:, :, -1]
    gt = np.tanh(pt.reshape(B, MD) + a_last @ (f64(A_th) * diag_mask()) + x @ f64(B_th) + f64(b_th))
    return gf, gi, gt


def setup_inputs():
    r = np.random.standard_normal
    u = mx_kscale(MD)
    ca, cb = 0.7 / np.sqrt(M), 0.7 / np.sqrt(N)
    x_t = bf(r((B, N)))
    m_t = bf(r((B, M)))
    a_t = bf(r((B, MD)))
    A_fg = bf(r((M, MD)) * ca)
    A_in = bf(r((M, MD)) * ca)
    A_th = bf(big_diag(r((M, MD)) * ca))
    A_pt_blk = bf(r((M, D, D)) * 0.4)
    B_fg0 = bf(r((N, MD)) * cb)
    B_in0 = bf(r((N, MD)) * cb)
    B_th0 = bf(r((N, MD)) * cb)
    b_fg = bf(r((1, MD)) * 0.3)
    b_in = bf(r((1, MD)) * 0.3)
    b_th = bf(r((1, MD)) * 0.3)
    g = bf(r((B, MD)) * np.exp2(np.random.randint(-12, 1, (B, 1))) * 8.0 * u)
    gf, gi, gt = gates(x_t, m_t, a_t, A_fg, A_in, A_th, A_pt_blk, B_fg0, B_in0, B_th0, b_fg, b_in, b_th)
    return {"x_t": x_t, "m_t": m_t, "a_t": a_t,
            "A_fg": A_fg, "A_in": A_in, "A_th": A_th, "A_pt_blk": A_pt_blk,
            "B_fg": bf(f64(B_fg0) / u), "B_in": bf(f64(B_in0) / u), "B_th": bf(f64(B_th0) / u),
            "b_fg": b_fg, "b_in": b_in, "b_th": b_th,
            "G_fg": np.asarray(gf, np.float32), "G_in": np.asarray(gi, np.float32), "G_th": np.asarray(gt, np.float32),
            "grad_out": g}


def reference(x_t, m_t, a_t, A_fg, A_in, A_th, A_pt_blk, B_fg, B_in, B_th, b_fg, b_in, b_th, G_fg, G_in, G_th, grad_out):
    g, a = f64(grad_out), f64(a_t)
    gf, gi, gt = f64(G_fg), f64(G_in), f64(G_th)
    d_fg = g * a * gf * (1.0 - gf)
    d_in = g * gt * gi * (1.0 - gi)
    d_th = g * gi * (1.0 - gt * gt)
    out = mxq(d_fg, 1, "e5m2") @ mxq(f64(B_fg), 1, "e4m3").T
    out = out + (mxq(d_in, 1, "e5m2") @ mxq(f64(B_in), 1, "e4m3").T)
    out = out + (mxq(d_th, 1, "e5m2") @ mxq(f64(B_th), 1, "e4m3").T)
    return out

@@ -1,0 +1,236 @@
+from contextlib import ExitStack
+
+import concourse.mybir as mybir
+from concourse.masks import make_identity
+
+F32 = mybir.dt.float32
+BF16 = mybir.dt.bfloat16
+U32 = mybir.dt.uint32
+U8 = mybir.dt.uint8
+E4M3_X4 = mybir.dt.float8_e4m3fn_x4
+E5M2_X4 = mybir.dt.float8_e5m2_x4
+ALU = mybir.AluOpType
+ACT = mybir.ActivationFunctionType
+
+P = 128
+PACK = 4
+K_PASS = P * PACK
+ROWS = 512
+FEATURES = 2048
+OUTS = 256
+ROW_TILES = ROWS // P
+OUT_TILES = OUTS // P
+ROUNDS = FEATURES // K_PASS
+UNITS = ROUNDS * ROW_TILES
+GATES = 3
+
+FLOPS = 2 * ROWS * OUTS * GATES * FEATURES
+BYTES = ROWS * FEATURES * (2 + 2 + GATES * 4) + GATES * OUTS * FEATURES * 2 + ROWS * OUTS * 4
+
+LOAD_BUFS = 8
+
+
+def tile_edrncell_pa_v_kernel(
+    tc, x_t, m_t, a_t, A_fg, A_in, A_th, A_pt_blk, B_fg, B_in, B_th, b_fg, b_in, b_th,
+    G_fg, G_in, G_th, grad_out, out,
+):
+    nc = tc.nc
+    weights = (B_fg, B_in, B_th)
+
+    with ExitStack() as stack:
+        stack.enter_context(tc.manual_schedule())
+        consts = stack.enter_context(tc.tile_pool(name="consts", bufs=1))
+        loads = stack.enter_context(tc.tile_pool(name="loads", bufs=LOAD_BUFS))
+        work = stack.enter_context(tc.tile_pool(name="work", bufs=3))
+        rounds = stack.enter_context(tc.tile_pool(name="rounds", bufs=2))
+        psum = stack.enter_context(tc.psum_pool(name="psum", bufs=1))
+
+        ident_f32 = consts.tile([P, P], F32)
+        make_identity(nc, ident_f32[:])
+        ident_bf16 = consts.tile([P, P], BF16)
+        make_identity(nc, ident_bf16[:])
+
+        w_codes = [
+            consts.tile([P, ROUNDS, OUTS], U32, name="w_codes%d" % x, align_bytes=64)
+            for x in range(GATES)
+        ]
+        w_scales = [
+            consts.tile([P, ROUNDS, OUTS], U8, name="w_scales%d" % x, align_bytes=64)
+            for x in range(GATES)
+        ]
+        acc = [psum.tile([P, ROWS], F32, name="acc%d" % j) for j in range(OUT_TILES)]
+
+        def load_unit(src, s, dtype, tag):
+            g, i = divmod(s, ROW_TILES)
+            natural = loads.tile([P, K_PASS], dtype, tag=tag, name=tag)
+            nc.sync.dma_start(
+                out=natural[:], in_=src[i * P : (i + 1) * P, g * K_PASS : (g + 1) * K_PASS]
+            )
+            return natural
+
+        def transpose_planes(dst, natural, ident):
+            for t in range(PACK):
+                nc.tensor.transpose(dst[:, t, :], natural[:, t * P : (t + 1) * P], ident[:])
+
+        def input_and_tanh_gates(s):
+            gate_th = load_unit(G_th, s, F32, "gate_th")
+            gate_in = load_unit(G_in, s, F32, "gate_in")
+            th_T = psum.tile([P, PACK, P], F32, tag="th_T", bufs=2)
+            transpose_planes(th_T, gate_th, ident_f32)
+            in_T = psum.tile([P, PACK, P], F32, tag="in_T", bufs=2)
+            transpose_planes(in_T, gate_in, ident_f32)
+            sq_th = work.tile([P, PACK, P], F32)
+            nc.scalar.activation(out=sq_th[:], in_=th_T[:], func=ACT.Square)
+            q_in = work.tile([P, PACK, P], F32)
+            nc.scalar.activation(out=q_in[:], in_=in_T[:], func=ACT.Square, bias=-0.5)
+            return th_T, in_T, sq_th, q_in
+
+        def forget_gate_and_gradient(s):
+            gate_fg = load_unit(G_fg, s, F32, "gate_fg")
+            grad = load_unit(grad_out, s, BF16, "grad")
+            state = load_unit(a_t, s, BF16, "state")
+            fg_T = psum.tile([P, PACK, P], F32, tag="fg_T_or_w_T")
+            transpose_planes(fg_T, gate_fg, ident_f32)
+            grad_state_T = psum.tile([P, 2, PACK, P], BF16)
+            transpose_planes(grad_state_T[:, 0], grad, ident_bf16)
+            transpose_planes(grad_state_T[:, 1], state, ident_bf16)
+            q_fg = work.tile([P, PACK, P], F32)
+            nc.scalar.activation(out=q_fg[:], in_=fg_T[:], func=ACT.Square, bias=-0.5)
+            grad_T = work.tile([P, PACK, P], BF16)
+            nc.scalar.copy(out=grad_T[:], in_=grad_state_T[:, 0])
+            return grad_state_T, q_fg, grad_T
+
+        def products(s, gates_T, rest_T, d):
+            th_T, in_T, sq_th, q_in = gates_T
+            grad_state_T, q_fg, grad_T = rest_T
+            d_fg, d_in, d_th = d
+            i = s % ROW_TILES
+            y = work.tile([P, PACK, P], F32)
+            nc.vector.scalar_tensor_tensor(
+                out=y[:], in0=sq_th[:], scalar=1.0, in1=in_T[:], op0=ALU.subtract, op1=ALU.mult
+            )
+            x_in = work.tile([P, PACK, P], F32)
+            nc.vector.scalar_tensor_tensor(
+                out=x_in[:], in0=q_in[:], scalar=0.25, in1=th_T[:], op0=ALU.subtract, op1=ALU.mult
+            )
+            nc.gpsimd.tensor_tensor(
+                out=d_in[:, i],
+                in0=x_in[:].rearrange("p t r -> p r t"),
+                in1=grad_T[:].rearrange("p t r -> p r t"),
+                op=ALU.mult,
+            )
+            x_fg = work.tile([P, PACK, P], F32)
+            nc.vector.scalar_tensor_tensor(
+                out=x_fg[:], in0=q_fg[:], scalar=0.25, in1=grad_state_T[:, 1],
+                op0=ALU.subtract, op1=ALU.mult,
+            )
+            nc.gpsimd.tensor_tensor(
+                out=d_fg[:, i],
+                in0=x_fg[:].rearrange("p t r -> p r t"),
+                in1=grad_T[:].rearrange("p t r -> p r t"),
+                op=ALU.mult,
+            )
+            nc.vector.tensor_tensor(
+                out=d_th[:, i],
+                in0=y[:].rearrange("p t r -> p r t"),
+                in1=grad_state_T[:, 0].rearrange("p t r -> p r t"),
+                op=ALU.mult,
+            )
+
+        def transpose_weight(x, g):
+            w_natural = loads.tile([P, OUT_TILES, K_PASS], BF16, bufs=3)
+            nc.sync.dma_start(
+                out=w_natural[:],
+                in_=weights[x].rearrange("(j n) k -> n j k", n=P)[
+                    :, :, g * K_PASS : (g + 1) * K_PASS
+                ],
+            )
+            w_T = psum.tile([P, PACK, OUT_TILES, P], BF16, tag="fg_T_or_w_T")
+            for j in range(OUT_TILES):
+                transpose_planes(w_T[:, :, j, :], w_natural[:, j, :], ident_bf16)
+            w_grouped = work.tile([P, OUTS, PACK], BF16, align_bytes=64)
+            nc.scalar.copy(out=w_grouped[:], in_=w_T[:].rearrange("p t j n -> p (j n) t"))
+            return w_grouped
+
+        def quantise_weight(x, g, w_grouped):
+            nc.vector.quantize_mx(
+                out=w_codes[x][:, g, :].bitcast(E4M3_X4),
+                scales=w_scales[x][:, g, :],
+                in_=w_grouped[:].rearrange("p n t -> p (n t)"),
+            )
+
+        def quantise_unit(s, d, d_codes, d_scales):
+            i = s % ROW_TILES
+            for x in range(GATES):
+                nc.vector.quantize_mx(
+                    out=d_codes[x][:, i * P : (i + 1) * P].bitcast(E5M2_X4),
+                    scales=d_scales[x][:, i * P : (i + 1) * P],
+                    in_=d[x][:, i].rearrange("p r t -> p (r t)"),
+                )
+
+        def multiply_round(g, d_codes, d_scales):
+            for j in range(OUT_TILES):
+                for x in range(GATES):
+                    nc.tensor.matmul_mx(
+                        out=acc[j][:],
+                        lhsT=w_codes[x][:, g, j * P : (j + 1) * P].bitcast(E4M3_X4),
+                        lhsT_scale=w_scales[x][:, g, j * P : (j + 1) * P],
+                        rhs=d_codes[x][:].bitcast(E5M2_X4),
+                        rhs_scale=d_scales[x][:],
+                        start=(g == 0 and x == 0),
+                        stop=(g == ROUNDS - 1 and x == GATES - 1),
+                    )
+
+        d = {}
+        d_codes = {}
+        d_scales = {}
+        w_waiting = None
+        gates_T = input_and_tanh_gates(0)
+        for s in range(UNITS):
+            g, i = divmod(s, ROW_TILES)
+            next_gates_T = input_and_tanh_gates(s + 1) if s + 1 < UNITS else None
+            rest_T = forget_gate_and_gradient(s)
+            if i == 0:
+                d[g] = [
+                    rounds.tile([P, ROW_TILES, P, PACK], BF16, name="d%d" % x, align_bytes=64)
+                    for x in range(GATES)
+                ]
+                d_codes[g] = [
+                    rounds.tile([P, ROWS], U32, name="d_codes%d" % x, align_bytes=64)
+                    for x in range(GATES)
+                ]
+                d_scales[g] = [
+                    rounds.tile([P, ROWS], U8, name="d_scales%d" % x, align_bytes=64)
+                    for x in range(GATES)
+                ]
+            products(s, gates_T, rest_T, d[g])
+            if s > 0:
+                g_before = (s - 1) // ROW_TILES
+                quantise_unit(s - 1, d[g_before], d_codes[g_before], d_scales[g_before])
+            if w_waiting is not None:
+                quantise_weight(*w_waiting)
+                w_waiting = None
+            if i < GATES:
+                w_waiting = (i, g, transpose_weight(i, g))
+            elif g > 0:
+                multiply_round(g - 1, d_codes[g - 1], d_scales[g - 1])
+            gates_T = next_gates_T
+        last = ROUNDS - 1
+        quantise_unit(UNITS - 1, d[last], d_codes[last], d_scales[last])
+        multiply_round(last, d_codes[last], d_scales[last])
+
+        out_T = [consts.tile([P, ROWS], F32, name="out_T%d" % j) for j in range(OUT_TILES)]
+        nc.scalar.mul(out=out_T[0][:], in_=acc[0][:], mul=-1.0)
+        nc.vector.tensor_scalar_mul(out=out_T[1][:], in0=acc[1][:], scalar1=-1.0)
+        for i in range(ROW_TILES):
+            out_ps = psum.tile([P, OUT_TILES, P], F32, tag="in_T", bufs=2)
+            for j in range(OUT_TILES):
+                nc.tensor.transpose(out_ps[:, j, :], out_T[j][:, i * P : (i + 1) * P], ident_f32[:])
+            out_sb = work.tile([P, OUT_TILES, P], F32)
+            if i % 2 == 0:
+                nc.scalar.copy(out=out_sb[:], in_=out_ps[:])
+            else:
+                nc.vector.tensor_copy(out=out_sb[:], in_=out_ps[:])
+            nc.sync.dma_start(
+                out=out[i * P : (i + 1) * P, :], in_=out_sb[:].rearrange("p j n -> p (j n)")
+            )

@@ -96,13 +96,12 @@ def tile_edrncell_pa_v_kernel(
             transpose_planes(grad_state_T[:, 1], state, ident_bf16)
             q_fg = work.tile([P, PACK, P], F32)
             nc.scalar.activation(out=q_fg[:], in_=fg_T[:], func=ACT.Square, bias=-0.5)
-            grad_T = work.tile([P, PACK, P], BF16)
-            nc.scalar.copy(out=grad_T[:], in_=grad_state_T[:, 0])
-            return grad_state_T, q_fg, grad_T
+            return grad_state_T, q_fg
 
         def products(s, gates_T, rest_T, d):
             th_T, in_T, sq_th, q_in = gates_T
-            grad_state_T, q_fg, grad_T = rest_T
+            grad_state_T, q_fg = rest_T
+            grad_T = grad_state_T[:, 0].rearrange("p t r -> p r t")
             d_fg, d_in, d_th = d
             i = s % ROW_TILES
             y = work.tile([P, PACK, P], F32)
@@ -113,28 +112,19 @@ def tile_edrncell_pa_v_kernel(
             nc.vector.scalar_tensor_tensor(
                 out=x_in[:], in0=q_in[:], scalar=0.25, in1=th_T[:], op0=ALU.subtract, op1=ALU.mult
             )
-            nc.gpsimd.tensor_tensor(
-                out=d_in[:, i],
-                in0=x_in[:].rearrange("p t r -> p r t"),
-                in1=grad_T[:].rearrange("p t r -> p r t"),
-                op=ALU.mult,
+            nc.vector.tensor_tensor(
+                out=d_in[:, i], in0=x_in[:].rearrange("p t r -> p r t"), in1=grad_T, op=ALU.mult
             )
             x_fg = work.tile([P, PACK, P], F32)
             nc.vector.scalar_tensor_tensor(
                 out=x_fg[:], in0=q_fg[:], scalar=0.25, in1=grad_state_T[:, 1],
                 op0=ALU.subtract, op1=ALU.mult,
             )
-            nc.gpsimd.tensor_tensor(
-                out=d_fg[:, i],
-                in0=x_fg[:].rearrange("p t r -> p r t"),
-                in1=grad_T[:].rearrange("p t r -> p r t"),
-                op=ALU.mult,
+            nc.vector.tensor_tensor(
+                out=d_fg[:, i], in0=x_fg[:].rearrange("p t r -> p r t"), in1=grad_T, op=ALU.mult
             )
             nc.vector.tensor_tensor(
-                out=d_th[:, i],
-                in0=y[:].rearrange("p t r -> p r t"),
-                in1=grad_state_T[:, 0].rearrange("p t r -> p r t"),
-                op=ALU.mult,
+                out=d_th[:, i], in0=y[:].rearrange("p t r -> p r t"), in1=grad_T, op=ALU.mult
             )
 
         def transpose_weight(x, g):

@@ -27,7 +27,8 @@ GATES = 3
 FLOPS = 2 * ROWS * OUTS * GATES * FEATURES
 BYTES = ROWS * FEATURES * (2 + 2 + GATES * 4) + GATES * OUTS * FEATURES * 2 + ROWS * OUTS * 4
 
-LOAD_BUFS = 8
+LOAD_BUFS = 6
+D_T_BANKS = 5
 
 
 def tile_edrncell_pa_v_kernel(
@@ -35,7 +36,7 @@ def tile_edrncell_pa_v_kernel(
     G_fg, G_in, G_th, grad_out, out,
 ):
     nc = tc.nc
-    weights = (B_fg, B_in, B_th)
+    weights = (B_fg, B_th, B_in)
 
     with ExitStack() as stack:
         stack.enter_context(tc.manual_schedule())
@@ -45,10 +46,10 @@ def tile_edrncell_pa_v_kernel(
         rounds = stack.enter_context(tc.tile_pool(name="rounds", bufs=2))
         psum = stack.enter_context(tc.psum_pool(name="psum", bufs=1))
 
-        ident_f32 = consts.tile([P, P], F32)
-        make_identity(nc, ident_f32[:])
         ident_bf16 = consts.tile([P, P], BF16)
         make_identity(nc, ident_bf16[:])
+        ident_f32 = consts.tile([P, P], F32)
+        make_identity(nc, ident_f32[:])
 
         w_codes = [
             consts.tile([P, ROUNDS, OUTS], U32, name="w_codes%d" % x, align_bytes=64)
@@ -68,64 +69,50 @@ def tile_edrncell_pa_v_kernel(
             )
             return natural
 
-        def transpose_planes(dst, natural, ident):
+        def transpose_planes(dst, natural):
             for t in range(PACK):
-                nc.tensor.transpose(dst[:, t, :], natural[:, t * P : (t + 1) * P], ident[:])
+                nc.tensor.transpose(dst[:, t, :], natural[:, t * P : (t + 1) * P], ident_bf16[:])
 
-        def input_and_tanh_gates(s):
-            gate_th = load_unit(G_th, s, F32, "gate_th")
-            gate_in = load_unit(G_in, s, F32, "gate_in")
-            th_T = psum.tile([P, PACK, P], F32, tag="th_T", bufs=2)
-            transpose_planes(th_T, gate_th, ident_f32)
-            in_T = psum.tile([P, PACK, P], F32, tag="in_T", bufs=2)
-            transpose_planes(in_T, gate_in, ident_f32)
-            sq_th = work.tile([P, PACK, P], F32)
-            nc.scalar.activation(out=sq_th[:], in_=th_T[:], func=ACT.Square)
-            q_in = work.tile([P, PACK, P], F32)
-            nc.scalar.activation(out=q_in[:], in_=in_T[:], func=ACT.Square, bias=-0.5)
-            return th_T, in_T, sq_th, q_in
-
-        def forget_gate_and_gradient(s):
-            gate_fg = load_unit(G_fg, s, F32, "gate_fg")
+        def load_and_square(s):
             grad = load_unit(grad_out, s, BF16, "grad")
             state = load_unit(a_t, s, BF16, "state")
-            fg_T = psum.tile([P, PACK, P], F32, tag="fg_T_or_w_T")
-            transpose_planes(fg_T, gate_fg, ident_f32)
-            grad_state_T = psum.tile([P, 2, PACK, P], BF16)
-            transpose_planes(grad_state_T[:, 0], grad, ident_bf16)
-            transpose_planes(grad_state_T[:, 1], state, ident_bf16)
-            q_fg = work.tile([P, PACK, P], F32)
-            nc.scalar.activation(out=q_fg[:], in_=fg_T[:], func=ACT.Square, bias=-0.5)
-            return grad_state_T, q_fg
+            gate_in = load_unit(G_in, s, F32, "gate_in")
+            gate_th = load_unit(G_th, s, F32, "gate_th")
+            gate_fg = load_unit(G_fg, s, F32, "gate_fg")
+            sq_th = work.tile([P, K_PASS], F32)
+            nc.scalar.activation(out=sq_th[:], in_=gate_th[:], func=ACT.Square)
+            q_fg = work.tile([P, K_PASS], F32)
+            nc.scalar.activation(out=q_fg[:], in_=gate_fg[:], func=ACT.Square, bias=-0.5)
+            return grad, state, gate_in, gate_th, sq_th, q_fg
 
-        def products(s, gates_T, rest_T, d):
-            th_T, in_T, sq_th, q_in = gates_T
-            grad_state_T, q_fg = rest_T
-            grad_T = grad_state_T[:, 0].rearrange("p t r -> p r t")
-            d_fg, d_in, d_th = d
+        def products(s, inputs, d_grouped):
+            grad, state, gate_in, gate_th, sq_th, q_fg = inputs
             i = s % ROW_TILES
-            y = work.tile([P, PACK, P], F32)
+            grad_state = work.tile([P, K_PASS], F32)
+            nc.vector.tensor_tensor(out=grad_state[:], in0=grad[:], in1=state[:], op=ALU.mult)
+            grad_in = work.tile([P, K_PASS], F32)
+            nc.vector.tensor_tensor(out=grad_in[:], in0=grad[:], in1=gate_in[:], op=ALU.mult)
+            in_th = work.tile([P, K_PASS], F32)
             nc.vector.scalar_tensor_tensor(
-                out=y[:], in0=sq_th[:], scalar=1.0, in1=in_T[:], op0=ALU.subtract, op1=ALU.mult
-            )
-            x_in = work.tile([P, PACK, P], F32)
-            nc.vector.scalar_tensor_tensor(
-                out=x_in[:], in0=q_in[:], scalar=0.25, in1=th_T[:], op0=ALU.subtract, op1=ALU.mult
-            )
-            nc.vector.tensor_tensor(
-                out=d_in[:, i], in0=x_in[:].rearrange("p t r -> p r t"), in1=grad_T, op=ALU.mult
-            )
-            x_fg = work.tile([P, PACK, P], F32)
-            nc.vector.scalar_tensor_tensor(
-                out=x_fg[:], in0=q_fg[:], scalar=0.25, in1=grad_state_T[:, 1],
+                out=in_th[:], in0=gate_in[:], scalar=1.0, in1=gate_th[:],
                 op0=ALU.subtract, op1=ALU.mult,
             )
-            nc.vector.tensor_tensor(
-                out=d_fg[:, i], in0=x_fg[:].rearrange("p t r -> p r t"), in1=grad_T, op=ALU.mult
+            d_fg = work.tile([P, K_PASS], BF16)
+            nc.vector.scalar_tensor_tensor(
+                out=d_fg[:], in0=q_fg[:], scalar=0.25, in1=grad_state[:],
+                op0=ALU.subtract, op1=ALU.mult,
             )
-            nc.vector.tensor_tensor(
-                out=d_th[:, i], in0=y[:].rearrange("p t r -> p r t"), in1=grad_T, op=ALU.mult
+            d_th = work.tile([P, K_PASS], BF16)
+            nc.vector.scalar_tensor_tensor(
+                out=d_th[:], in0=sq_th[:], scalar=1.0, in1=grad_in[:],
+                op0=ALU.subtract, op1=ALU.mult,
             )
+            d_in = work.tile([P, K_PASS], BF16)
+            nc.vector.tensor_tensor(out=d_in[:], in0=grad_in[:], in1=in_th[:], op=ALU.mult)
+            for x, d_natural in enumerate((d_fg, d_th, d_in)):
+                d_T = psum.tile([P, PACK, P], BF16, bufs=D_T_BANKS)
+                transpose_planes(d_T, d_natural)
+                nc.scalar.copy(out=d_grouped[x][:, i], in_=d_T[:].rearrange("p t r -> p r t"))
 
         def transpose_weight(x, g):
             w_natural = loads.tile([P, OUT_TILES, K_PASS], BF16, bufs=3)
@@ -135,9 +122,9 @@ def tile_edrncell_pa_v_kernel(
                     :, :, g * K_PASS : (g + 1) * K_PASS
                 ],
             )
-            w_T = psum.tile([P, PACK, OUT_TILES, P], BF16, tag="fg_T_or_w_T")
+            w_T = psum.tile([P, PACK, OUT_TILES, P], BF16)
             for j in range(OUT_TILES):
-                transpose_planes(w_T[:, :, j, :], w_natural[:, j, :], ident_bf16)
+                transpose_planes(w_T[:, :, j, :], w_natural[:, j, :])
             w_grouped = work.tile([P, OUTS, PACK], BF16, align_bytes=64)
             nc.scalar.copy(out=w_grouped[:], in_=w_T[:].rearrange("p t j n -> p (j n) t"))
             return w_grouped
@@ -149,18 +136,18 @@ def tile_edrncell_pa_v_kernel(
                 in_=w_grouped[:].rearrange("p n t -> p (n t)"),
             )
 
-        def quantise_unit(s, d, d_codes, d_scales):
+        def quantise_unit(s, d_grouped, d_codes, d_scales):
             i = s % ROW_TILES
             for x in range(GATES):
                 nc.vector.quantize_mx(
                     out=d_codes[x][:, i * P : (i + 1) * P].bitcast(E5M2_X4),
                     scales=d_scales[x][:, i * P : (i + 1) * P],
-                    in_=d[x][:, i].rearrange("p r t -> p (r t)"),
+                    in_=d_grouped[x][:, i].rearrange("p r t -> p (r t)"),
                 )
 
         def multiply_round(g, d_codes, d_scales):
-            for j in range(OUT_TILES):
-                for x in range(GATES):
+            for x in range(GATES):
+                for j in range(OUT_TILES):
                     nc.tensor.matmul_mx(
                         out=acc[j][:],
                         lhsT=w_codes[x][:, g, j * P : (j + 1) * P].bitcast(E4M3_X4),
@@ -171,18 +158,17 @@ def tile_edrncell_pa_v_kernel(
                         stop=(g == ROUNDS - 1 and x == GATES - 1),
                     )
 
-        d = {}
+        d_grouped = {}
         d_codes = {}
         d_scales = {}
         w_waiting = None
-        gates_T = input_and_tanh_gates(0)
+        inputs = load_and_square(0)
         for s in range(UNITS):
             g, i = divmod(s, ROW_TILES)
-            next_gates_T = input_and_tanh_gates(s + 1) if s + 1 < UNITS else None
-            rest_T = forget_gate_and_gradient(s)
+            next_inputs = load_and_square(s + 1) if s + 1 < UNITS else None
             if i == 0:
-                d[g] = [
-                    rounds.tile([P, ROW_TILES, P, PACK], BF16, name="d%d" % x, align_bytes=64)
+                d_grouped[g] = [
+                    rounds.tile([P, ROW_TILES, P, PACK], BF16, name="d_grouped%d" % x, align_bytes=64)
                     for x in range(GATES)
                 ]
                 d_codes[g] = [
@@ -193,27 +179,27 @@ def tile_edrncell_pa_v_kernel(
                     rounds.tile([P, ROWS], U8, name="d_scales%d" % x, align_bytes=64)
                     for x in range(GATES)
                 ]
-            products(s, gates_T, rest_T, d[g])
+            products(s, inputs, d_grouped[g])
             if s > 0:
                 g_before = (s - 1) // ROW_TILES
-                quantise_unit(s - 1, d[g_before], d_codes[g_before], d_scales[g_before])
+                quantise_unit(s - 1, d_grouped[g_before], d_codes[g_before], d_scales[g_before])
             if w_waiting is not None:
                 quantise_weight(*w_waiting)
                 w_waiting = None
+            if i == 0 and g > 0:
+                multiply_round(g - 1, d_codes[g - 1], d_scales[g - 1])
             if i < GATES:
                 w_waiting = (i, g, transpose_weight(i, g))
-            elif g > 0:
-                multiply_round(g - 1, d_codes[g - 1], d_scales[g - 1])
-            gates_T = next_gates_T
+            inputs = next_inputs
         last = ROUNDS - 1
-        quantise_unit(UNITS - 1, d[last], d_codes[last], d_scales[last])
+        quantise_unit(UNITS - 1, d_grouped[last], d_codes[last], d_scales[last])
         multiply_round(last, d_codes[last], d_scales[last])
 
         out_T = [consts.tile([P, ROWS], F32, name="out_T%d" % j) for j in range(OUT_TILES)]
         nc.scalar.mul(out=out_T[0][:], in_=acc[0][:], mul=-1.0)
         nc.vector.tensor_scalar_mul(out=out_T[1][:], in0=acc[1][:], scalar1=-1.0)
         for i in range(ROW_TILES):
-            out_ps = psum.tile([P, OUT_TILES, P], F32, tag="in_T", bufs=2)
+            out_ps = psum.tile([P, OUT_TILES, P], F32, tag="d_T", bufs=D_T_BANKS)
             for j in range(OUT_TILES):
                 nc.tensor.transpose(out_ps[:, j, :], out_T[j][:, i * P : (i + 1) * P], ident_f32[:])
             out_sb = work.tile([P, OUT_TILES, P], F32)

@@ -7,6 +7,7 @@ F32 = mybir.dt.float32
 BF16 = mybir.dt.bfloat16
 U32 = mybir.dt.uint32
 U8 = mybir.dt.uint8
+I32 = mybir.dt.int32
 E4M3_X4 = mybir.dt.float8_e4m3fn_x4
 E5M2_X4 = mybir.dt.float8_e5m2_x4
 ALU = mybir.AluOpType
@@ -20,6 +21,7 @@ FEATURES = 2048
 OUTS = 256
 ROW_TILES = ROWS // P
 OUT_TILES = OUTS // P
+N_MOVING = 2 * OUTS
 ROUNDS = FEATURES // K_PASS
 UNITS = ROUNDS * ROW_TILES
 GATES = 3
@@ -28,7 +30,16 @@ FLOPS = 2 * ROWS * OUTS * GATES * FEATURES
 BYTES = ROWS * FEATURES * (2 + 2 + GATES * 4) + GATES * OUTS * FEATURES * 2 + ROWS * OUTS * 4
 
 LOAD_BUFS = 6
-D_T_BANKS = 5
+D_T_BANKS = 3
+CODE_BUFS = 4
+
+
+def weight_step(x, g):
+    return GATES * g + x
+
+
+def multiply_step(s):
+    return max(s + 1, weight_step(GATES - 1, s // ROW_TILES) + 1)
 
 
 def tile_edrncell_pa_v_kernel(
@@ -43,23 +54,25 @@ def tile_edrncell_pa_v_kernel(
         consts = stack.enter_context(tc.tile_pool(name="consts", bufs=1))
         loads = stack.enter_context(tc.tile_pool(name="loads", bufs=LOAD_BUFS))
         work = stack.enter_context(tc.tile_pool(name="work", bufs=3))
-        rounds = stack.enter_context(tc.tile_pool(name="rounds", bufs=2))
+        codes = stack.enter_context(tc.tile_pool(name="codes", bufs=CODE_BUFS))
         psum = stack.enter_context(tc.psum_pool(name="psum", bufs=1))
 
         ident_bf16 = consts.tile([P, P], BF16)
         make_identity(nc, ident_bf16[:])
-        ident_f32 = consts.tile([P, P], F32)
-        make_identity(nc, ident_f32[:])
 
         w_codes = [
-            consts.tile([P, ROUNDS, OUTS], U32, name="w_codes%d" % x, align_bytes=64)
+            consts.tile([P, ROUNDS + 1, OUTS], U32, name="w_codes%d" % x, align_bytes=64)
             for x in range(GATES)
         ]
         w_scales = [
-            consts.tile([P, ROUNDS, OUTS], U8, name="w_scales%d" % x, align_bytes=64)
+            consts.tile([P, ROUNDS + 1, OUTS], U8, name="w_scales%d" % x, align_bytes=64)
             for x in range(GATES)
         ]
-        acc = [psum.tile([P, ROWS], F32, name="acc%d" % j) for j in range(OUT_TILES)]
+        for x in range(GATES):
+            nc.vector.memset(w_codes[x][:, 0, :].bitcast(I32), 0)
+            nc.vector.memset(w_scales[x][:, 0, :].bitcast(I32), 0)
+        acc = [psum.tile([P, N_MOVING], F32, name="acc%d" % i) for i in range(ROW_TILES)]
+        out_sb = consts.tile([P, ROW_TILES, OUTS], F32)
 
         def load_unit(src, s, dtype, tag):
             g, i = divmod(s, ROW_TILES)
@@ -85,9 +98,8 @@ def tile_edrncell_pa_v_kernel(
             nc.scalar.activation(out=q_fg[:], in_=gate_fg[:], func=ACT.Square, bias=-0.5)
             return grad, state, gate_in, gate_th, sq_th, q_fg
 
-        def products(s, inputs, d_grouped):
+        def products(inputs):
             grad, state, gate_in, gate_th, sq_th, q_fg = inputs
-            i = s % ROW_TILES
             grad_state = work.tile([P, K_PASS], F32)
             nc.vector.tensor_tensor(out=grad_state[:], in0=grad[:], in1=state[:], op=ALU.mult)
             grad_in = work.tile([P, K_PASS], F32)
@@ -109,10 +121,14 @@ def tile_edrncell_pa_v_kernel(
             )
             d_in = work.tile([P, K_PASS], BF16)
             nc.vector.tensor_tensor(out=d_in[:], in0=grad_in[:], in1=in_th[:], op=ALU.mult)
+            d_grouped = []
             for x, d_natural in enumerate((d_fg, d_th, d_in)):
                 d_T = psum.tile([P, PACK, P], BF16, bufs=D_T_BANKS)
                 transpose_planes(d_T, d_natural)
-                nc.scalar.copy(out=d_grouped[x][:, i], in_=d_T[:].rearrange("p t r -> p r t"))
+                grouped = work.tile([P, P, PACK], BF16, name="d_grouped%d" % x, align_bytes=64)
+                nc.scalar.copy(out=grouped[:], in_=d_T[:].rearrange("p t r -> p r t"))
+                d_grouped.append(grouped)
+            return d_grouped
 
         def transpose_weight(x, g):
             w_natural = loads.tile([P, OUT_TILES, K_PASS], BF16, bufs=3)
@@ -131,82 +147,61 @@ def tile_edrncell_pa_v_kernel(
 
         def quantise_weight(x, g, w_grouped):
             nc.vector.quantize_mx(
-                out=w_codes[x][:, g, :].bitcast(E4M3_X4),
-                scales=w_scales[x][:, g, :],
+                out=w_codes[x][:, g + 1, :].bitcast(E4M3_X4),
+                scales=w_scales[x][:, g + 1, :],
                 in_=w_grouped[:].rearrange("p n t -> p (n t)"),
             )
 
-        def quantise_unit(s, d_grouped, d_codes, d_scales):
-            i = s % ROW_TILES
+        def quantise_unit(d_grouped):
+            d_codes = []
             for x in range(GATES):
+                words = codes.tile([P, P], U32, name="d_words%d" % x, align_bytes=64)
+                scales = codes.tile([P, P], U8, name="d_scales%d" % x, align_bytes=64)
                 nc.vector.quantize_mx(
-                    out=d_codes[x][:, i * P : (i + 1) * P].bitcast(E5M2_X4),
-                    scales=d_scales[x][:, i * P : (i + 1) * P],
-                    in_=d_grouped[x][:, i].rearrange("p r t -> p (r t)"),
+                    out=words[:].bitcast(E5M2_X4),
+                    scales=scales[:],
+                    in_=d_grouped[x][:].rearrange("p r t -> p (r t)"),
                 )
+                d_codes.append((words, scales))
+            return d_codes
 
-        def multiply_round(g, d_codes, d_scales):
+        def multiply_unit(s, d_codes):
+            g, i = divmod(s, ROW_TILES)
             for x in range(GATES):
-                for j in range(OUT_TILES):
-                    nc.tensor.matmul_mx(
-                        out=acc[j][:],
-                        lhsT=w_codes[x][:, g, j * P : (j + 1) * P].bitcast(E4M3_X4),
-                        lhsT_scale=w_scales[x][:, g, j * P : (j + 1) * P],
-                        rhs=d_codes[x][:].bitcast(E5M2_X4),
-                        rhs_scale=d_scales[x][:],
-                        start=(g == 0 and x == 0),
-                        stop=(g == ROUNDS - 1 and x == GATES - 1),
-                    )
+                words, scales = d_codes[x]
+                nc.tensor.matmul_mx(
+                    out=acc[i][:],
+                    lhsT=words[:].bitcast(E5M2_X4),
+                    lhsT_scale=scales[:],
+                    rhs=w_codes[x][:, g : g + 2, :].rearrange("p g n -> p (g n)").bitcast(E4M3_X4),
+                    rhs_scale=w_scales[x][:, g : g + 2, :].rearrange("p g n -> p (g n)"),
+                    start=(g == 0 and x == 0),
+                    stop=(g == ROUNDS - 1 and x == GATES - 1),
+                )
+            if g == ROUNDS - 1:
+                nc.scalar.mul(out=out_sb[:, i, :], in_=acc[i][:, OUTS:N_MOVING], mul=-1.0)
 
+        inputs = {0: load_and_square(0)}
         d_grouped = {}
         d_codes = {}
-        d_scales = {}
         w_waiting = None
-        inputs = load_and_square(0)
-        for s in range(UNITS):
-            g, i = divmod(s, ROW_TILES)
-            next_inputs = load_and_square(s + 1) if s + 1 < UNITS else None
-            if i == 0:
-                d_grouped[g] = [
-                    rounds.tile([P, ROW_TILES, P, PACK], BF16, name="d_grouped%d" % x, align_bytes=64)
-                    for x in range(GATES)
-                ]
-                d_codes[g] = [
-                    rounds.tile([P, ROWS], U32, name="d_codes%d" % x, align_bytes=64)
-                    for x in range(GATES)
-                ]
-                d_scales[g] = [
-                    rounds.tile([P, ROWS], U8, name="d_scales%d" % x, align_bytes=64)
-                    for x in range(GATES)
-                ]
-            products(s, inputs, d_grouped[g])
-            if s > 0:
-                g_before = (s - 1) // ROW_TILES
-                quantise_unit(s - 1, d_grouped[g_before], d_codes[g_before], d_scales[g_before])
+        for u in range(UNITS + 1):
+            if u + 1 < UNITS:
+                inputs[u + 1] = load_and_square(u + 1)
+            if u < UNITS:
+                d_grouped[u] = products(inputs[u])
+            if u > 0:
+                d_codes[u - 1] = quantise_unit(d_grouped[u - 1])
             if w_waiting is not None:
                 quantise_weight(*w_waiting)
                 w_waiting = None
-            if i == 0 and g > 0:
-                multiply_round(g - 1, d_codes[g - 1], d_scales[g - 1])
-            if i < GATES:
-                w_waiting = (i, g, transpose_weight(i, g))
-            inputs = next_inputs
-        last = ROUNDS - 1
-        quantise_unit(UNITS - 1, d_grouped[last], d_codes[last], d_scales[last])
-        multiply_round(last, d_codes[last], d_scales[last])
+            for s in range(UNITS):
+                if multiply_step(s) == u:
+                    multiply_unit(s, d_codes[s])
+            for g in range(ROUNDS):
+                for x in range(GATES):
+                    if weight_step(x, g) == u:
+                        w_waiting = (x, g, transpose_weight(x, g))
 
-        out_T = [consts.tile([P, ROWS], F32, name="out_T%d" % j) for j in range(OUT_TILES)]
-        nc.scalar.mul(out=out_T[0][:], in_=acc[0][:], mul=-1.0)
-        nc.vector.tensor_scalar_mul(out=out_T[1][:], in0=acc[1][:], scalar1=-1.0)
         for i in range(ROW_TILES):
-            out_ps = psum.tile([P, OUT_TILES, P], F32, tag="d_T", bufs=D_T_BANKS)
-            for j in range(OUT_TILES):
-                nc.tensor.transpose(out_ps[:, j, :], out_T[j][:, i * P : (i + 1) * P], ident_f32[:])
-            out_sb = work.tile([P, OUT_TILES, P], F32)
-            if i % 2 == 0:
-                nc.scalar.copy(out=out_sb[:], in_=out_ps[:])
-            else:
-                nc.vector.tensor_copy(out=out_sb[:], in_=out_ps[:])
-            nc.sync.dma_start(
-                out=out[i * P : (i + 1) * P, :], in_=out_sb[:].rearrange("p j n -> p (j n)")
-            )
+            nc.sync.dma_start(out=out[i * P : (i + 1) * P, :], in_=out_sb[:, i, :])

@@ -47,7 +47,7 @@ def tile_edrncell_pa_v_kernel(
     G_fg, G_in, G_th, grad_out, out,
 ):
     nc = tc.nc
-    weights = (B_fg, B_th, B_in)
+    weights = (B_in, B_th, B_fg)
 
     with ExitStack() as stack:
         stack.enter_context(tc.manual_schedule())
@@ -88,9 +88,9 @@ def tile_edrncell_pa_v_kernel(
 
         def load_and_square(s):
             grad = load_unit(grad_out, s, BF16, "grad")
-            state = load_unit(a_t, s, BF16, "state")
             gate_in = load_unit(G_in, s, F32, "gate_in")
             gate_th = load_unit(G_th, s, F32, "gate_th")
+            state = load_unit(a_t, s, BF16, "state")
             gate_fg = load_unit(G_fg, s, F32, "gate_fg")
             sq_th = work.tile([P, K_PASS], F32)
             nc.scalar.activation(out=sq_th[:], in_=gate_th[:], func=ACT.Square)
@@ -100,8 +100,6 @@ def tile_edrncell_pa_v_kernel(
 
         def products(inputs):
             grad, state, gate_in, gate_th, sq_th, q_fg = inputs
-            grad_state = work.tile([P, K_PASS], F32)
-            nc.vector.tensor_tensor(out=grad_state[:], in0=grad[:], in1=state[:], op=ALU.mult)
             grad_in = work.tile([P, K_PASS], F32)
             nc.vector.tensor_tensor(out=grad_in[:], in0=grad[:], in1=gate_in[:], op=ALU.mult)
             in_th = work.tile([P, K_PASS], F32)
@@ -109,20 +107,22 @@ def tile_edrncell_pa_v_kernel(
                 out=in_th[:], in0=gate_in[:], scalar=1.0, in1=gate_th[:],
                 op0=ALU.subtract, op1=ALU.mult,
             )
-            d_fg = work.tile([P, K_PASS], BF16)
-            nc.vector.scalar_tensor_tensor(
-                out=d_fg[:], in0=q_fg[:], scalar=0.25, in1=grad_state[:],
-                op0=ALU.subtract, op1=ALU.mult,
-            )
+            grad_state = work.tile([P, K_PASS], F32)
+            nc.vector.tensor_tensor(out=grad_state[:], in0=grad[:], in1=state[:], op=ALU.mult)
+            d_in = work.tile([P, K_PASS], BF16)
+            nc.vector.tensor_tensor(out=d_in[:], in0=grad_in[:], in1=in_th[:], op=ALU.mult)
             d_th = work.tile([P, K_PASS], BF16)
             nc.vector.scalar_tensor_tensor(
                 out=d_th[:], in0=sq_th[:], scalar=1.0, in1=grad_in[:],
                 op0=ALU.subtract, op1=ALU.mult,
             )
-            d_in = work.tile([P, K_PASS], BF16)
-            nc.vector.tensor_tensor(out=d_in[:], in0=grad_in[:], in1=in_th[:], op=ALU.mult)
+            d_fg = work.tile([P, K_PASS], BF16)
+            nc.vector.scalar_tensor_tensor(
+                out=d_fg[:], in0=q_fg[:], scalar=0.25, in1=grad_state[:],
+                op0=ALU.subtract, op1=ALU.mult,
+            )
             d_grouped = []
-            for x, d_natural in enumerate((d_fg, d_th, d_in)):
+            for x, d_natural in enumerate((d_in, d_th, d_fg)):
                 d_T = psum.tile([P, PACK, P], BF16, bufs=D_T_BANKS)
                 transpose_planes(d_T, d_natural)
                 grouped = work.tile([P, P, PACK], BF16, name="d_grouped%d" % x, align_bytes=64)
@@ -195,13 +195,13 @@ def tile_edrncell_pa_v_kernel(
             if w_waiting is not None:
                 quantise_weight(*w_waiting)
                 w_waiting = None
-            for s in range(UNITS):
-                if multiply_step(s) == u:
-                    multiply_unit(s, d_codes[s])
             for g in range(ROUNDS):
                 for x in range(GATES):
                     if weight_step(x, g) == u:
                         w_waiting = (x, g, transpose_weight(x, g))
+            for s in range(UNITS):
+                if multiply_step(s) == u:
+                    multiply_unit(s, d_codes[s])
 
         for i in range(ROW_TILES):
             nc.sync.dma_start(out=out[i * P : (i + 1) * P, :], in_=out_sb[:, i, :])

@@ -15,6 +15,8 @@ ACT = mybir.ActivationFunctionType
 
 P = 128
 PACK = 4
+PAIR = 2
+HALVES = PACK // PAIR
 K_PASS = P * PACK
 ROWS = 512
 FEATURES = 2048
@@ -57,8 +59,8 @@ def tile_edrncell_pa_v_kernel(
         codes = stack.enter_context(tc.tile_pool(name="codes", bufs=CODE_BUFS))
         psum = stack.enter_context(tc.psum_pool(name="psum", bufs=1))
 
-        ident_bf16 = consts.tile([P, P], BF16)
-        make_identity(nc, ident_bf16[:])
+        ident_f32 = consts.tile([P, P], F32)
+        make_identity(nc, ident_f32[:])
 
         w_codes = [
             consts.tile([P, ROUNDS + 1, OUTS], U32, name="w_codes%d" % x, align_bytes=64)
@@ -82,9 +84,10 @@ def tile_edrncell_pa_v_kernel(
             )
             return natural
 
-        def transpose_planes(dst, natural):
-            for t in range(PACK):
-                nc.tensor.transpose(dst[:, t, :], natural[:, t * P : (t + 1) * P], ident_bf16[:])
+        def transpose_words(dst, natural):
+            words = natural.bitcast(F32)
+            for h in range(HALVES):
+                nc.tensor.transpose(dst[:, h, :], words[:, h * P : (h + 1) * P], ident_f32[:])
 
         def load_and_square(s):
             grad = load_unit(grad_out, s, BF16, "grad")
@@ -123,10 +126,15 @@ def tile_edrncell_pa_v_kernel(
             )
             d_grouped = []
             for x, d_natural in enumerate((d_in, d_th, d_fg)):
-                d_T = psum.tile([P, PACK, P], BF16, bufs=D_T_BANKS)
-                transpose_planes(d_T, d_natural)
+                d_T = psum.tile([P, HALVES, P], F32, bufs=D_T_BANKS)
+                transpose_words(d_T, d_natural[:])
                 grouped = work.tile([P, P, PACK], BF16, name="d_grouped%d" % x, align_bytes=64)
-                nc.scalar.copy(out=grouped[:], in_=d_T[:].rearrange("p t r -> p r t"))
+                nc.scalar.copy(
+                    out=grouped[:].rearrange("p r t -> p (r t)").bitcast(F32).rearrange(
+                        "p (r h) -> p r h", h=HALVES
+                    ),
+                    in_=d_T[:].rearrange("p h r -> p r h"),
+                )
                 d_grouped.append(grouped)
             return d_grouped
 
@@ -138,11 +146,16 @@ def tile_edrncell_pa_v_kernel(
                     :, :, g * K_PASS : (g + 1) * K_PASS
                 ],
             )
-            w_T = psum.tile([P, PACK, OUT_TILES, P], BF16)
+            w_T = psum.tile([P, HALVES, OUT_TILES, P], F32)
             for j in range(OUT_TILES):
-                transpose_planes(w_T[:, :, j, :], w_natural[:, j, :])
+                transpose_words(w_T[:, :, j, :], w_natural[:, j, :])
             w_grouped = work.tile([P, OUTS, PACK], BF16, align_bytes=64)
-            nc.scalar.copy(out=w_grouped[:], in_=w_T[:].rearrange("p t j n -> p (j n) t"))
+            nc.scalar.copy(
+                out=w_grouped[:].rearrange("p n t -> p (n t)").bitcast(F32).rearrange(
+                    "p (n h) -> p n h", h=HALVES
+                ),
+                in_=w_T[:].rearrange("p h j n -> p (j n) h"),
+            )
             return w_grouped
 
         def quantise_weight(x, g, w_grouped):

@@ -25,23 +25,33 @@ ROW_TILES = ROWS // P
 OUT_TILES = OUTS // P
 N_MOVING = 2 * OUTS
 ROUNDS = FEATURES // K_PASS
-UNITS = ROUNDS * ROW_TILES
 GATES = 3
 
 FLOPS = 2 * ROWS * OUTS * GATES * FEATURES
 BYTES = ROWS * FEATURES * (2 + 2 + GATES * 4) + GATES * OUTS * FEATURES * 2 + ROWS * OUTS * 4
 
-LOAD_BUFS = 6
+ROUND_SPLITS = ((1, 1, 2), (2, 2), (2, 2), (2, 1, 1))
+UNIT_LIST = tuple(
+    (g, sum(split[:n]), size) for g, split in enumerate(ROUND_SPLITS) for n, size in enumerate(split)
+)
+UNITS = len(UNIT_LIST)
+LOAD_BUFS = 4
 D_T_BANKS = 3
 CODE_BUFS = 4
 
 
 def weight_step(x, g):
-    return GATES * g + x
+    place = GATES * g + x
+    row_tiles_before = 0
+    for u, (unit_round, first, size) in enumerate(UNIT_LIST):
+        row_tiles_before += size
+        if place < row_tiles_before:
+            return u
+    raise ValueError("more weight tensors than row tiles")
 
 
 def multiply_step(s):
-    return max(s + 1, weight_step(GATES - 1, s // ROW_TILES) + 1)
+    return max(s + 1, weight_step(GATES - 1, UNIT_LIST[s][0]) + 1)
 
 
 def tile_edrncell_pa_v_kernel(
@@ -77,10 +87,13 @@ def tile_edrncell_pa_v_kernel(
         out_sb = consts.tile([P, ROW_TILES, OUTS], F32)
 
         def load_unit(src, s, dtype, tag):
-            g, i = divmod(s, ROW_TILES)
-            natural = loads.tile([P, K_PASS], dtype, tag=tag, name=tag)
+            g, first, size = UNIT_LIST[s]
+            natural = loads.tile([P, size, K_PASS], dtype, tag=tag, name=tag)
             nc.sync.dma_start(
-                out=natural[:], in_=src[i * P : (i + 1) * P, g * K_PASS : (g + 1) * K_PASS]
+                out=natural[:],
+                in_=src.rearrange("(i p) k -> p i k", p=P)[
+                    :, first : first + size, g * K_PASS : (g + 1) * K_PASS
+                ],
             )
             return natural
 
@@ -95,45 +108,49 @@ def tile_edrncell_pa_v_kernel(
             gate_th = load_unit(G_th, s, F32, "gate_th")
             state = load_unit(a_t, s, BF16, "state")
             gate_fg = load_unit(G_fg, s, F32, "gate_fg")
-            sq_th = work.tile([P, K_PASS], F32)
+            size = UNIT_LIST[s][2]
+            sq_th = work.tile([P, size, K_PASS], F32)
             nc.scalar.activation(out=sq_th[:], in_=gate_th[:], func=ACT.Square)
-            q_fg = work.tile([P, K_PASS], F32)
+            q_fg = work.tile([P, size, K_PASS], F32)
             nc.scalar.activation(out=q_fg[:], in_=gate_fg[:], func=ACT.Square, bias=-0.5)
             return grad, state, gate_in, gate_th, sq_th, q_fg
 
-        def products(inputs):
+        def products(size, inputs):
             grad, state, gate_in, gate_th, sq_th, q_fg = inputs
-            grad_in = work.tile([P, K_PASS], F32)
+            grad_in = work.tile([P, size, K_PASS], F32)
             nc.vector.tensor_tensor(out=grad_in[:], in0=grad[:], in1=gate_in[:], op=ALU.mult)
-            in_th = work.tile([P, K_PASS], F32)
+            in_th = work.tile([P, size, K_PASS], F32)
             nc.vector.scalar_tensor_tensor(
                 out=in_th[:], in0=gate_in[:], scalar=1.0, in1=gate_th[:],
                 op0=ALU.subtract, op1=ALU.mult,
             )
-            grad_state = work.tile([P, K_PASS], F32)
+            grad_state = work.tile([P, size, K_PASS], F32)
             nc.vector.tensor_tensor(out=grad_state[:], in0=grad[:], in1=state[:], op=ALU.mult)
-            d_in = work.tile([P, K_PASS], BF16)
+            d_in = work.tile([P, size, K_PASS], BF16)
             nc.vector.tensor_tensor(out=d_in[:], in0=grad_in[:], in1=in_th[:], op=ALU.mult)
-            d_th = work.tile([P, K_PASS], BF16)
+            d_th = work.tile([P, size, K_PASS], BF16)
             nc.vector.scalar_tensor_tensor(
                 out=d_th[:], in0=sq_th[:], scalar=1.0, in1=grad_in[:],
                 op0=ALU.subtract, op1=ALU.mult,
             )
-            d_fg = work.tile([P, K_PASS], BF16)
+            d_fg = work.tile([P, size, K_PASS], BF16)
             nc.vector.scalar_tensor_tensor(
                 out=d_fg[:], in0=q_fg[:], scalar=0.25, in1=grad_state[:],
                 op0=ALU.subtract, op1=ALU.mult,
             )
             d_grouped = []
             for x, d_natural in enumerate((d_in, d_th, d_fg)):
-                d_T = psum.tile([P, HALVES, P], F32, bufs=D_T_BANKS)
-                transpose_words(d_T, d_natural[:])
-                grouped = work.tile([P, P, PACK], BF16, name="d_grouped%d" % x, align_bytes=64)
+                d_T = psum.tile([P, size, HALVES, P], F32, bufs=D_T_BANKS)
+                for n in range(size):
+                    transpose_words(d_T[:, n], d_natural[:, n, :])
+                grouped = work.tile(
+                    [P, size * P * PACK], BF16, name="d_grouped%d" % x, align_bytes=64
+                )
                 nc.scalar.copy(
-                    out=grouped[:].rearrange("p r t -> p (r t)").bitcast(F32).rearrange(
-                        "p (r h) -> p r h", h=HALVES
+                    out=grouped[:].bitcast(F32).rearrange(
+                        "p (n r h) -> p n r h", n=size, h=HALVES
                     ),
-                    in_=d_T[:].rearrange("p h r -> p r h"),
+                    in_=d_T[:].rearrange("p n h r -> p n r h"),
                 )
                 d_grouped.append(grouped)
             return d_grouped
@@ -165,53 +182,55 @@ def tile_edrncell_pa_v_kernel(
                 in_=w_grouped[:].rearrange("p n t -> p (n t)"),
             )
 
-        def quantise_unit(d_grouped):
+        def quantise_unit(size, d_grouped):
             d_codes = []
             for x in range(GATES):
-                words = codes.tile([P, P], U32, name="d_words%d" % x, align_bytes=64)
-                scales = codes.tile([P, P], U8, name="d_scales%d" % x, align_bytes=64)
+                words = codes.tile([P, size * P], U32, name="d_words%d" % x, align_bytes=64)
+                scales = codes.tile([P, size * P], U8, name="d_scales%d" % x, align_bytes=64)
                 nc.vector.quantize_mx(
-                    out=words[:].bitcast(E5M2_X4),
-                    scales=scales[:],
-                    in_=d_grouped[x][:].rearrange("p r t -> p (r t)"),
+                    out=words[:].bitcast(E5M2_X4), scales=scales[:], in_=d_grouped[x][:]
                 )
                 d_codes.append((words, scales))
             return d_codes
 
         def multiply_unit(s, d_codes):
-            g, i = divmod(s, ROW_TILES)
-            for x in range(GATES):
-                words, scales = d_codes[x]
-                nc.tensor.matmul_mx(
-                    out=acc[i][:],
-                    lhsT=words[:].bitcast(E5M2_X4),
-                    lhsT_scale=scales[:],
-                    rhs=w_codes[x][:, g : g + 2, :].rearrange("p g n -> p (g n)").bitcast(E4M3_X4),
-                    rhs_scale=w_scales[x][:, g : g + 2, :].rearrange("p g n -> p (g n)"),
-                    start=(g == 0 and x == 0),
-                    stop=(g == ROUNDS - 1 and x == GATES - 1),
-                )
-            if g == ROUNDS - 1:
-                nc.scalar.mul(out=out_sb[:, i, :], in_=acc[i][:, OUTS:N_MOVING], mul=-1.0)
+            g, first, size = UNIT_LIST[s]
+            for n in range(size):
+                i = first + n
+                for x in range(GATES):
+                    words, scales = d_codes[x]
+                    nc.tensor.matmul_mx(
+                        out=acc[i][:],
+                        lhsT=words[:, n * P : (n + 1) * P].bitcast(E5M2_X4),
+                        lhsT_scale=scales[:, n * P : (n + 1) * P],
+                        rhs=w_codes[x][:, g : g + 2, :].rearrange("p g n -> p (g n)").bitcast(
+                            E4M3_X4
+                        ),
+                        rhs_scale=w_scales[x][:, g : g + 2, :].rearrange("p g n -> p (g n)"),
+                        start=(g == 0 and x == 0),
+                        stop=(g == ROUNDS - 1 and x == GATES - 1),
+                    )
+                if g == ROUNDS - 1:
+                    nc.scalar.mul(out=out_sb[:, i, :], in_=acc[i][:, OUTS:N_MOVING], mul=-1.0)
 
         inputs = {0: load_and_square(0)}
         d_grouped = {}
         d_codes = {}
-        w_waiting = None
+        w_waiting = []
         for u in range(UNITS + 1):
             if u + 1 < UNITS:
                 inputs[u + 1] = load_and_square(u + 1)
             if u < UNITS:
-                d_grouped[u] = products(inputs[u])
+                d_grouped[u] = products(UNIT_LIST[u][2], inputs[u])
             if u > 0:
-                d_codes[u - 1] = quantise_unit(d_grouped[u - 1])
-            if w_waiting is not None:
-                quantise_weight(*w_waiting)
-                w_waiting = None
+                d_codes[u - 1] = quantise_unit(UNIT_LIST[u - 1][2], d_grouped[u - 1])
+            for waiting in w_waiting:
+                quantise_weight(*waiting)
+            w_waiting = []
             for g in range(ROUNDS):
                 for x in range(GATES):
                     if weight_step(x, g) == u:
-                        w_waiting = (x, g, transpose_weight(x, g))
+                        w_waiting.append((x, g, transpose_weight(x, g)))
             for s in range(UNITS):
                 if multiply_step(s) == u:
                     multiply_unit(s, d_codes[s])

from contextlib import ExitStack

import concourse.mybir as mybir
from concourse.masks import make_identity

F32 = mybir.dt.float32
BF16 = mybir.dt.bfloat16
U32 = mybir.dt.uint32
U8 = mybir.dt.uint8
I32 = mybir.dt.int32
E4M3_X4 = mybir.dt.float8_e4m3fn_x4
E5M2_X4 = mybir.dt.float8_e5m2_x4
ALU = mybir.AluOpType
ACT = mybir.ActivationFunctionType

P = 128
PACK = 4
PAIR = 2
HALVES = PACK // PAIR
K_PASS = P * PACK
ROWS = 512
FEATURES = 2048
OUTS = 256
ROW_TILES = ROWS // P
OUT_TILES = OUTS // P
N_MOVING = 2 * OUTS
ROUNDS = FEATURES // K_PASS
GATES = 3

FLOPS = 2 * ROWS * OUTS * GATES * FEATURES
BYTES = ROWS * FEATURES * (2 + 2 + GATES * 4) + GATES * OUTS * FEATURES * 2 + ROWS * OUTS * 4

ROUND_SPLITS = ((1, 1, 2), (2, 2), (2, 2), (2, 1, 1))
UNIT_LIST = tuple(
    (g, sum(split[:n]), size) for g, split in enumerate(ROUND_SPLITS) for n, size in enumerate(split)
)
UNITS = len(UNIT_LIST)
LOAD_BUFS = 4
D_T_BANKS = 3
CODE_BUFS = 4


def weight_step(x, g):
    place = GATES * g + x
    row_tiles_before = 0
    for u, (unit_round, first, size) in enumerate(UNIT_LIST):
        row_tiles_before += size
        if place < row_tiles_before:
            return u
    raise ValueError("more weight tensors than row tiles")


def multiply_step(s):
    return max(s + 1, weight_step(GATES - 1, UNIT_LIST[s][0]) + 1)


def tile_edrncell_pa_v_kernel(
    tc, x_t, m_t, a_t, A_fg, A_in, A_th, A_pt_blk, B_fg, B_in, B_th, b_fg, b_in, b_th,
    G_fg, G_in, G_th, grad_out, out,
):
    nc = tc.nc
    weights = (B_in, B_th, B_fg)

    with ExitStack() as stack:
        stack.enter_context(tc.manual_schedule())
        consts = stack.enter_context(tc.tile_pool(name="consts", bufs=1))
        loads = stack.enter_context(tc.tile_pool(name="loads", bufs=LOAD_BUFS))
        work = stack.enter_context(tc.tile_pool(name="work", bufs=3))
        codes = stack.enter_context(tc.tile_pool(name="codes", bufs=CODE_BUFS))
        psum = stack.enter_context(tc.psum_pool(name="psum", bufs=1))

        ident_f32 = consts.tile([P, P], F32)
        make_identity(nc, ident_f32[:])

        w_codes = [
            consts.tile([P, ROUNDS + 1, OUTS], U32, name="w_codes%d" % x, align_bytes=64)
            for x in range(GATES)
        ]
        w_scales = [
            consts.tile([P, ROUNDS + 1, OUTS], U8, name="w_scales%d" % x, align_bytes=64)
            for x in range(GATES)
        ]
        for x in range(GATES):
            nc.vector.memset(w_codes[x][:, 0, :].bitcast(I32), 0)
            nc.vector.memset(w_scales[x][:, 0, :].bitcast(I32), 0)
        acc = [psum.tile([P, N_MOVING], F32, name="acc%d" % i) for i in range(ROW_TILES)]
        out_sb = consts.tile([P, ROW_TILES, OUTS], F32)

        def load_unit(src, s, dtype, tag):
            g, first, size = UNIT_LIST[s]
            natural = loads.tile([P, size, K_PASS], dtype, tag=tag, name=tag)
            nc.sync.dma_start(
                out=natural[:],
                in_=src.rearrange("(i p) k -> p i k", p=P)[
                    :, first : first + size, g * K_PASS : (g + 1) * K_PASS
                ],
            )
            return natural

        def transpose_words(dst, natural):
            words = natural.bitcast(F32)
            for h in range(HALVES):
                nc.tensor.transpose(dst[:, h, :], words[:, h * P : (h + 1) * P], ident_f32[:])

        def load_and_square(s):
            grad = load_unit(grad_out, s, BF16, "grad")
            gate_in = load_unit(G_in, s, F32, "gate_in")
            gate_th = load_unit(G_th, s, F32, "gate_th")
            state = load_unit(a_t, s, BF16, "state")
            gate_fg = load_unit(G_fg, s, F32, "gate_fg")
            size = UNIT_LIST[s][2]
            sq_th = work.tile([P, size, K_PASS], F32)
            nc.scalar.activation(out=sq_th[:], in_=gate_th[:], func=ACT.Square)
            q_fg = work.tile([P, size, K_PASS], F32)
            nc.scalar.activation(out=q_fg[:], in_=gate_fg[:], func=ACT.Square, bias=-0.5)
            return grad, state, gate_in, gate_th, sq_th, q_fg

        def products(size, inputs):
            grad, state, gate_in, gate_th, sq_th, q_fg = inputs
            grad_in = work.tile([P, size, K_PASS], F32)
            nc.vector.tensor_tensor(out=grad_in[:], in0=grad[:], in1=gate_in[:], op=ALU.mult)
            in_th = work.tile([P, size, K_PASS], F32)
            nc.vector.scalar_tensor_tensor(
                out=in_th[:], in0=gate_in[:], scalar=1.0, in1=gate_th[:],
                op0=ALU.subtract, op1=ALU.mult,
            )
            grad_state = work.tile([P, size, K_PASS], F32)
            nc.vector.tensor_tensor(out=grad_state[:], in0=grad[:], in1=state[:], op=ALU.mult)
            d_in = work.tile([P, size, K_PASS], BF16)
            nc.vector.tensor_tensor(out=d_in[:], in0=grad_in[:], in1=in_th[:], op=ALU.mult)
            d_th = work.tile([P, size, K_PASS], BF16)
            nc.vector.scalar_tensor_tensor(
                out=d_th[:], in0=sq_th[:], scalar=1.0, in1=grad_in[:],
                op0=ALU.subtract, op1=ALU.mult,
            )
            d_fg = work.tile([P, size, K_PASS], BF16)
            nc.vector.scalar_tensor_tensor(
                out=d_fg[:], in0=q_fg[:], scalar=0.25, in1=grad_state[:],
                op0=ALU.subtract, op1=ALU.mult,
            )
            d_grouped = []
            for x, d_natural in enumerate((d_in, d_th, d_fg)):
                d_T = psum.tile([P, size, HALVES, P], F32, bufs=D_T_BANKS)
                for n in range(size):
                    transpose_words(d_T[:, n], d_natural[:, n, :])
                grouped = work.tile(
                    [P, size * P * PACK], BF16, name="d_grouped%d" % x, align_bytes=64
                )
                nc.scalar.copy(
                    out=grouped[:].bitcast(F32).rearrange(
                        "p (n r h) -> p n r h", n=size, h=HALVES
                    ),
                    in_=d_T[:].rearrange("p n h r -> p n r h"),
                )
                d_grouped.append(grouped)
            return d_grouped

        def transpose_weight(x, g):
            w_natural = loads.tile([P, OUT_TILES, K_PASS], BF16, bufs=3)
            nc.sync.dma_start(
                out=w_natural[:],
                in_=weights[x].rearrange("(j n) k -> n j k", n=P)[
                    :, :, g * K_PASS : (g + 1) * K_PASS
                ],
            )
            w_T = psum.tile([P, HALVES, OUT_TILES, P], F32)
            for j in range(OUT_TILES):
                transpose_words(w_T[:, :, j, :], w_natural[:, j, :])
            w_grouped = work.tile([P, OUTS, PACK], BF16, align_bytes=64)
            nc.scalar.copy(
                out=w_grouped[:].rearrange("p n t -> p (n t)").bitcast(F32).rearrange(
                    "p (n h) -> p n h", h=HALVES
                ),
                in_=w_T[:].rearrange("p h j n -> p (j n) h"),
            )
            return w_grouped

        def quantise_weight(x, g, w_grouped):
            nc.vector.quantize_mx(
                out=w_codes[x][:, g + 1, :].bitcast(E4M3_X4),
                scales=w_scales[x][:, g + 1, :],
                in_=w_grouped[:].rearrange("p n t -> p (n t)"),
            )

        def quantise_unit(size, d_grouped):
            d_codes = []
            for x in range(GATES):
                words = codes.tile([P, size * P], U32, name="d_words%d" % x, align_bytes=64)
                scales = codes.tile([P, size * P], U8, name="d_scales%d" % x, align_bytes=64)
                nc.vector.quantize_mx(
                    out=words[:].bitcast(E5M2_X4), scales=scales[:], in_=d_grouped[x][:]
                )
                d_codes.append((words, scales))
            return d_codes

        def multiply_unit(s, d_codes):
            g, first, size = UNIT_LIST[s]
            for n in range(size):
                i = first + n
                for x in range(GATES):
                    words, scales = d_codes[x]
                    nc.tensor.matmul_mx(
                        out=acc[i][:],
                        lhsT=words[:, n * P : (n + 1) * P].bitcast(E5M2_X4),
                        lhsT_scale=scales[:, n * P : (n + 1) * P],
                        rhs=w_codes[x][:, g : g + 2, :].rearrange("p g n -> p (g n)").bitcast(
                            E4M3_X4
                        ),
                        rhs_scale=w_scales[x][:, g : g + 2, :].rearrange("p g n -> p (g n)"),
                        start=(g == 0 and x == 0),
                        stop=(g == ROUNDS - 1 and x == GATES - 1),
                    )
                if g == ROUNDS - 1:
                    nc.scalar.mul(out=out_sb[:, i, :], in_=acc[i][:, OUTS:N_MOVING], mul=-1.0)

        inputs = {0: load_and_square(0)}
        d_grouped = {}
        d_codes = {}
        w_waiting = []
        for u in range(UNITS + 1):
            if u + 1 < UNITS:
                inputs[u + 1] = load_and_square(u + 1)
            if u < UNITS:
                d_grouped[u] = products(UNIT_LIST[u][2], inputs[u])
            if u > 0:
                d_codes[u - 1] = quantise_unit(UNIT_LIST[u - 1][2], d_grouped[u - 1])
            for waiting in w_waiting:
                quantise_weight(*waiting)
            w_waiting = []
            for g in range(ROUNDS):
                for x in range(GATES):
                    if weight_step(x, g) == u:
                        w_waiting.append((x, g, transpose_weight(x, g)))
            for s in range(UNITS):
                if multiply_step(s) == u:
                    multiply_unit(s, d_codes[s])

        for i in range(ROW_TILES):
            nc.sync.dma_start(out=out[i * P : (i + 1) * P, :], in_=out_sb[:, i, :])
